import numpy as np
import ml_dtypes


def mxq(x, axis, fmt="e4m3"):
    dtype, down = {"e4m3": (ml_dtypes.float8_e4m3fn, 7), "e5m2": (ml_dtypes.float8_e5m2, 14)}[fmt]
    v = np.moveaxis(np.asarray(x, np.float32).astype(ml_dtypes.bfloat16).astype(np.float64), axis, -1)
    blocks = v.reshape(v.shape[:-1] + (-1, 32))
    amax = np.abs(blocks).max(-1, keepdims=True)
    byte = np.maximum(np.where(amax > 0, np.frexp(amax)[1] - 1 + 127, 0) - down, 1)
    scale = np.exp2(byte - 127.0)
    codes = (blocks / scale).astype(np.float32).astype(dtype).astype(np.float64)
    return np.moveaxis((codes * scale).reshape(v.shape), -1, axis)


WIDE = False


def mx_kscale(k):
    if not WIDE:
        return np.ones(k)
    levels = np.array([10, -10, 5, -5, 0])
    a = np.random.permutation(np.resize(levels, k // 512 * 4)).reshape(k // 512, 4)
    idx = np.arange(k)
    return np.exp2(a[idx // 512, idx % 128 // 32])


BF16 = ml_dtypes.bfloat16


def bf(x):
    return np.asarray(x, np.float32).astype(BF16)


def f64(x):
    return np.asarray(x).astype(np.float64)


E2M1 = np.array([0.0, 0.5, 1.0, 1.5, 2.0, 3.0, 4.0, 6.0, -0.0, -0.5, -1.0, -1.5, -2.0, -3.0, -4.0, -6.0])


def pack_weight(w, fmt):
    k, n = w.shape
    w = f64(bf(w)).reshape(k // 32, 32, n)
    amax = np.abs(w).max(1)
    if fmt == "e4m3":
        byte = np.frexp(amax)[1] - 1 + 127 - 7
    else:
        mant, ex = np.frexp(amax / 6.0)
        byte = np.where(mant > 0.5, ex, ex - 1) + 127
    byte = np.clip(np.where(amax > 0, byte, 1), 1, 254)
    scaled = (w * np.exp2(127.0 - byte)[:, None, :]).reshape(k, n).astype(np.float32)
    by_word = np.ascontiguousarray(scaled.reshape(k // 512, 128, 4, n).transpose(0, 1, 3, 2))
    if fmt == "e4m3":
        words = by_word.astype(ml_dtypes.float8_e4m3fn).view(np.uint8)
    else:
        c = by_word.astype(ml_dtypes.float4_e2m1fn).view(np.uint8) & 0xF
        words = c[..., 0::2] | (c[..., 1::2] << 4)
    return np.ascontiguousarray(words), np.ascontiguousarray(byte.astype(np.uint8).reshape(k // 512, 16, n))


def unpack_weight(words, scales, fmt):
    g, p, n, _ = words.shape
    if fmt == "e4m3":
        vals = np.ascontiguousarray(words).view(ml_dtypes.float8_e4m3fn).astype(np.float64)
    else:
        nib = np.empty((g, p, n, 4), np.uint8)
        nib[..., 0::2] = words & 0xF
        nib[..., 1::2] = words >> 4
        vals = E2M1[nib]
    vals = vals * np.repeat(np.exp2(scales.astype(np.float64) - 127.0), 8, axis=1)[..., None]
    return vals.transpose(0, 1, 3, 2).reshape(g * 512, n)

def pack4(w):
    words, scales = pack_weight(w, "e2m1")
    return words.reshape(words.shape[0], 128, -1), scales


def unpack4(words, scales):
    return unpack_weight(words.reshape(words.shape[0], 128, -1, 2), scales, "e2m1")


B, T, D, H, HD = 2, 64, 8192, 8, 128
E = H * HD


def rope(u):
    inv_freq = 1.0 / (10000.0 ** (f64(np.arange(0, HD, 2)) / HD))
    pe = f64(np.arange(T))[:, None] * inv_freq[None, :]
    pe = np.repeat(pe, 2, axis=-1)
    u1 = u[..., 0::2]
    u2 = u[..., 1::2]
    rot = np.stack((-u2, u1), axis=-1).reshape(u.shape)
    return u * np.cos(pe) + rot * np.sin(pe)


def split_heads(u):
    return u.reshape(B, T, H, HD).transpose(0, 2, 1, 3)


def setup_inputs():
    s = mx_kscale(D)
    x = bf(np.random.standard_normal((B, T, D)) * s)
    words, scales = pack4(np.random.standard_normal((D, 3 * E)) / np.sqrt(D) / s[:, None])
    return {"x": x, "w_qkv_words": words, "w_qkv_scales": scales}


def reference(x, w_qkv_words, w_qkv_scales):
    qkv = mxq(f64(x), 2, "e4m3") @ unpack4(w_qkv_words, w_qkv_scales)
    q, k, v = np.split(qkv, 3, axis=2)
    q, k, v = split_heads(q), split_heads(k), split_heads(v)
    return rope(q), rope(k), v

@@ -1,0 +1,249 @@
+import math
+from contextlib import ExitStack
+
+import concourse.mybir as mybir
+from concourse.masks import make_identity
+
+F32 = mybir.dt.float32
+BF16 = mybir.dt.bfloat16
+I32 = mybir.dt.int32
+U32 = mybir.dt.uint32
+U8 = mybir.dt.uint8
+FP8X4 = mybir.dt.float8_e4m3fn_x4
+FP4X4 = mybir.dt.float4_e2m1fn_x4
+ALU = mybir.AluOpType
+ACT = mybir.ActivationFunctionType
+
+P = 128
+PACK = 4
+K_PASS = P * PACK
+
+BATCH, SEQ, D_MODEL, HEADS, HEAD_DIM = 2, 64, 8192, 8, 128
+TOKENS = BATCH * SEQ
+WIDTH = HEADS * HEAD_DIM
+OUTPUTS = 3
+N_OUT = OUTPUTS * WIDTH
+GROUPS = D_MODEL // K_PASS
+
+BANK_COLS = 512
+BANKS = N_OUT // BANK_COLS
+BANKS_PER_OUTPUT = WIDTH // BANK_COLS
+HEADS_PER_BANK = BANK_COLS // HEAD_DIM
+ROTATED_BANKS = 2 * BANKS_PER_OUTPUT
+PAIRS = HEAD_DIM // 2
+
+WORD_BYTES = 2
+ROW_BYTES = WORD_BYTES * N_OUT
+
+X_PIECES = 4
+GROUPS_PER_QUANTISE = 4
+GROUPS_PER_STRETCH = 8
+GROUPS_PER_SCALE_DMA = 4
+SPLIT_GROUPS = 6
+
+ROPE_BASE = 10000.0
+ROUND_MAGIC = 1.5 * 2.0**23
+TWO_PI_HIGH = 6.28125
+TWO_PI_LOW = 2.0 * math.pi - TWO_PI_HIGH
+
+FLOPS = 2 * TOKENS * D_MODEL * N_OUT
+
+
+def build_rope_tables(nc, pool):
+    freq = pool.tile([P, HEAD_DIM], F32)
+    nc.vector.memset(freq[:, 0:2], 1.0)
+    done = 2
+    while done < HEAD_DIM:
+        ratio = ROPE_BASE ** (-float(done) / HEAD_DIM)
+        nc.vector.tensor_scalar_mul(out=freq[:, done : 2 * done], in0=freq[:, 0:done], scalar1=ratio)
+        done *= 2
+
+    token_index = pool.tile([P, 1], I32)
+    nc.gpsimd.iota(token_index[:], pattern=[[0, 1]], base=0, channel_multiplier=1)
+    position_int = pool.tile([P, 1], I32)
+    nc.vector.tensor_single_scalar(out=position_int[:], in_=token_index[:], scalar=SEQ - 1, op=ALU.bitwise_and)
+    position = pool.tile([P, 1], F32)
+    nc.vector.tensor_copy(out=position[:], in_=position_int[:])
+
+    angle = pool.tile([P, HEAD_DIM], F32)
+    nc.vector.tensor_scalar_mul(out=angle[:], in0=freq[:], scalar1=position[:, 0:1])
+
+    shifted = pool.tile([P, HEAD_DIM], F32)
+    nc.vector.tensor_scalar(
+        out=shifted[:], in0=angle[:], scalar1=1.0 / (2.0 * math.pi), scalar2=ROUND_MAGIC, op0=ALU.mult, op1=ALU.add
+    )
+    turns = pool.tile([P, HEAD_DIM], F32)
+    nc.vector.tensor_scalar_sub(out=turns[:], in0=shifted[:], scalar1=ROUND_MAGIC)
+    coarse = pool.tile([P, HEAD_DIM], F32)
+    nc.vector.scalar_tensor_tensor(
+        out=coarse[:], in0=turns[:], scalar=-TWO_PI_HIGH, in1=angle[:], op0=ALU.mult, op1=ALU.add
+    )
+    reduced = pool.tile([P, HEAD_DIM], F32)
+    nc.vector.scalar_tensor_tensor(
+        out=reduced[:], in0=turns[:], scalar=-TWO_PI_LOW, in1=coarse[:], op0=ALU.mult, op1=ALU.add
+    )
+    magnitude = pool.tile([P, HEAD_DIM], F32)
+    nc.vector.scalar_tensor_tensor(
+        out=magnitude[:], in0=reduced[:], scalar=-1.0, in1=reduced[:], op0=ALU.mult, op1=ALU.max
+    )
+    cos_arg = pool.tile([P, HEAD_DIM], F32)
+    nc.vector.tensor_scalar(
+        out=cos_arg[:], in0=magnitude[:], scalar1=-1.0, scalar2=math.pi / 2.0, op0=ALU.mult, op1=ALU.add
+    )
+
+    cos_pairs = pool.tile([P, HEAD_DIM], F32)
+    nc.scalar.activation(out=cos_pairs[:], in_=cos_arg[:], func=ACT.Sin)
+    sin_signed = pool.tile([P, 2, PAIRS], F32)
+    one_of_each_pair = reduced[:, 0:HEAD_DIM:2]
+    nc.scalar.activation(out=sin_signed[:, 0, :], in_=one_of_each_pair, func=ACT.Sin, scale=-1.0)
+    nc.scalar.activation(out=sin_signed[:, 1, :], in_=one_of_each_pair, func=ACT.Sin)
+    return cos_pairs, sin_signed
+
+
+def tile_selfattention_pa_k_kernel(tc, x, w_qkv_words, w_qkv_scales, out_0, out_1, out_2):
+    nc = tc.nc
+    outs = (out_0, out_1, out_2)
+
+    with ExitStack() as ctx:
+        ctx.enter_context(tc.manual_schedule())
+        keep = ctx.enter_context(tc.tile_pool(name="keep", bufs=1))
+        work = ctx.enter_context(tc.tile_pool(name="work", bufs=2))
+        psum_xt = ctx.enter_context(tc.psum_pool(name="psum_xt", bufs=2))
+        psum_acc = ctx.enter_context(tc.psum_pool(name="psum_acc", bufs=1))
+
+        x_sb = keep.tile([P, D_MODEL], BF16)
+        x_grouped = keep.tile([P, GROUPS, PACK * TOKENS], BF16, align_bytes=64)
+        x_codes = keep.tile([P, GROUPS, TOKENS], U32, align_bytes=64)
+        x_scales = keep.tile([P, GROUPS, TOKENS], U8, align_bytes=64)
+        w_words = keep.tile([P, GROUPS, ROW_BYTES], U8, align_bytes=64)
+        w_scales = keep.tile([P, GROUPS, N_OUT], U8, align_bytes=64)
+        identity = keep.tile([P, P], F32)
+        make_identity(nc, identity[:])
+
+        def load_scales(first_group):
+            stretch = slice(first_group, first_group + GROUPS_PER_STRETCH)
+            nc.vector.memset(w_scales[:, stretch, :].rearrange("p g n -> p (g n)").bitcast(I32), 0)
+            for g in range(first_group, first_group + GROUPS_PER_STRETCH, GROUPS_PER_SCALE_DMA):
+                for q in range(8):
+                    partition = 32 * (q // 4) + q % 4
+                    nc.sync.dma_start(
+                        out=w_scales[partition:P:64, g : g + GROUPS_PER_SCALE_DMA, :].bitcast(I32),
+                        in_=w_qkv_scales[g : g + GROUPS_PER_SCALE_DMA, q:16:8, :]
+                        .rearrange("g q n -> q g n")
+                        .bitcast(I32),
+                    )
+
+        def load_words(g, first_byte, last_byte):
+            nc.sync.dma_start(
+                out=w_words[:, g, first_byte:last_byte].bitcast(I32),
+                in_=w_qkv_words[g, :, first_byte:last_byte].bitcast(I32),
+            )
+
+        x_rows = x.rearrange("b t d -> (b t) d")
+        piece = D_MODEL // X_PIECES
+        for i in range(X_PIECES):
+            nc.sync.dma_start(out=x_sb[:, i * piece : (i + 1) * piece], in_=x_rows[:, i * piece : (i + 1) * piece])
+        first_split_group = GROUPS - SPLIT_GROUPS
+        for first_group in range(0, GROUPS, GROUPS_PER_STRETCH):
+            load_scales(first_group)
+            for g in range(first_group, min(first_group + GROUPS_PER_STRETCH, first_split_group)):
+                load_words(g, 0, ROW_BYTES)
+        for output in range(OUTPUTS):
+            for g in range(first_split_group, GROUPS):
+                load_words(g, output * WORD_BYTES * WIDTH, (output + 1) * WORD_BYTES * WIDTH)
+
+        x_words = x_sb[:].bitcast(F32)
+        words_per_group = K_PASS // 2
+
+        def transpose_two_groups(first_group, copy):
+            xt = psum_xt.tile([P, 2, 2, TOKENS], F32)
+            for i in range(2):
+                start = (first_group + i) * words_per_group
+                for u in range(2):
+                    nc.tensor.transpose(xt[:, i, u, :], x_words[:, start + u : start + words_per_group : 2], identity[:])
+            copy(
+                out=x_grouped[:, first_group : first_group + 2, :].bitcast(F32).rearrange("p g (m u) -> p g m u", u=2),
+                in_=xt[:].rearrange("p g u m -> p g m u"),
+            )
+
+        def quantise(first_group):
+            these = slice(first_group, first_group + GROUPS_PER_QUANTISE)
+            nc.vector.quantize_mx(
+                out=x_codes[:, these, :].rearrange("p g m -> p (g m)").bitcast(FP8X4),
+                scales=x_scales[:, these, :].rearrange("p g m -> p (g m)"),
+                in_=x_grouped[:, these, :].rearrange("p g c -> p (g c)"),
+            )
+
+        for first_group in range(0, GROUPS + GROUPS_PER_QUANTISE, GROUPS_PER_QUANTISE):
+            if first_group < GROUPS:
+                transpose_two_groups(first_group, nc.vector.tensor_copy)
+                transpose_two_groups(first_group + 2, nc.scalar.copy)
+            if first_group > 0:
+                quantise(first_group - GROUPS_PER_QUANTISE)
+
+        cos_pairs, sin_signed = build_rope_tables(nc, keep)
+
+        acc = [psum_acc.tile([P, BANK_COLS], F32, name="acc%d" % n) for n in range(BANKS)]
+        result = [keep.tile([P, BANK_COLS], F32, name="result%d" % n) for n in range(BANKS)]
+
+        def multiply(g, n):
+            nc.tensor.matmul_mx(
+                out=acc[n][:],
+                lhsT=x_codes[:, g, :].bitcast(FP8X4),
+                lhsT_scale=x_scales[:, g, :],
+                rhs=w_words[:, g, n * WORD_BYTES * BANK_COLS : (n + 1) * WORD_BYTES * BANK_COLS].bitcast(FP4X4),
+                rhs_scale=w_scales[:, g, n * BANK_COLS : (n + 1) * BANK_COLS],
+                start=(g == 0),
+                stop=(g == GROUPS - 1),
+            )
+
+        def rotate(n):
+            by_head = "p (h d) -> p h d"
+            cos_part = work.tile([P, BANK_COLS], F32)
+            nc.vector.tensor_tensor(
+                out=cos_part[:].rearrange(by_head, d=HEAD_DIM),
+                in0=acc[n][:].rearrange(by_head, d=HEAD_DIM),
+                in1=cos_pairs[:].unsqueeze(1).to_broadcast([P, HEADS_PER_BANK, HEAD_DIM]),
+                op=ALU.mult,
+            )
+            u_planes = acc[n][:].rearrange("p (c j) -> p j c", j=2)
+            sin_part = work.tile([P, 2, BANK_COLS // 2], F32)
+            for j in range(2):
+                nc.vector.tensor_tensor(
+                    out=sin_part[:, j, :].rearrange(by_head, d=PAIRS),
+                    in0=u_planes[:, 1 - j, :].rearrange(by_head, d=PAIRS),
+                    in1=sin_signed[:, j, :].unsqueeze(1).to_broadcast([P, HEADS_PER_BANK, PAIRS]),
+                    op=ALU.mult,
+                )
+            nc.vector.tensor_tensor(
+                out=result[n][:].rearrange("p (c j) -> p c j", j=2),
+                in0=cos_part[:].rearrange("p (c j) -> p c j", j=2),
+                in1=sin_part[:].rearrange("p j c -> p c j"),
+                op=ALU.add,
+            )
+
+        def store(n):
+            output, half = divmod(n, BANKS_PER_OUTPUT)
+            heads = slice(half * HEADS_PER_BANK, (half + 1) * HEADS_PER_BANK)
+            for b in range(BATCH):
+                nc.sync.dma_start(
+                    out=outs[output][b, heads].rearrange("h t d -> t h d"),
+                    in_=result[n][b * SEQ : (b + 1) * SEQ, :].rearrange("t (h d) -> t h d", d=HEAD_DIM),
+                )
+
+        for g in range(first_split_group):
+            for n in range(BANKS):
+                multiply(g, n)
+        for output in range(OUTPUTS):
+            banks = range(output * BANKS_PER_OUTPUT, (output + 1) * BANKS_PER_OUTPUT)
+            for g in range(first_split_group, GROUPS):
+                for n in banks:
+                    multiply(g, n)
+            for n in banks:
+                if n < ROTATED_BANKS:
+                    rotate(n)
+                elif n % 2 == 0:
+                    nc.scalar.copy(out=result[n][:], in_=acc[n][:])
+                else:
+                    nc.vector.tensor_copy(out=result[n][:], in_=acc[n][:])
+                store(n)

@@ -58,10 +58,10 @@ def build_rope_tables(nc, pool):
         nc.vector.tensor_scalar_mul(out=freq[:, done : 2 * done], in0=freq[:, 0:done], scalar1=ratio)
         done *= 2
 
-    token_index = pool.tile([P, 1], I32)
-    nc.gpsimd.iota(token_index[:], pattern=[[0, 1]], base=0, channel_multiplier=1)
+    partition_index = pool.tile([P, 1], I32)
+    nc.gpsimd.iota(partition_index[:], pattern=[[0, 1]], base=0, channel_multiplier=1)
     position_int = pool.tile([P, 1], I32)
-    nc.vector.tensor_single_scalar(out=position_int[:], in_=token_index[:], scalar=SEQ - 1, op=ALU.bitwise_and)
+    nc.vector.tensor_single_scalar(out=position_int[:], in_=partition_index[:], scalar=1, op=ALU.logical_shift_right)
     position = pool.tile([P, 1], F32)
     nc.vector.tensor_copy(out=position[:], in_=position_int[:])
 
@@ -139,10 +139,12 @@ def tile_selfattention_pa_k_kernel(tc, x, w_qkv_words, w_qkv_scales, out_0, out_
                 in_=w_qkv_words[g, :, first_byte:last_byte].bitcast(I32),
             )
 
-        x_rows = x.rearrange("b t d -> (b t) d")
         piece = D_MODEL // X_PIECES
         for i in range(X_PIECES):
-            nc.sync.dma_start(out=x_sb[:, i * piece : (i + 1) * piece], in_=x_rows[:, i * piece : (i + 1) * piece])
+            for b in range(BATCH):
+                nc.sync.dma_start(
+                    out=x_sb[b:P:BATCH, i * piece : (i + 1) * piece], in_=x[b, :, i * piece : (i + 1) * piece]
+                )
         first_split_group = GROUPS - SPLIT_GROUPS
         for first_group in range(0, GROUPS, GROUPS_PER_STRETCH):
             load_scales(first_group)
@@ -228,7 +230,7 @@ def tile_selfattention_pa_k_kernel(tc, x, w_qkv_words, w_qkv_scales, out_0, out_
             for b in range(BATCH):
                 nc.sync.dma_start(
                     out=outs[output][b, heads].rearrange("h t d -> t h d"),
-                    in_=result[n][b * SEQ : (b + 1) * SEQ, :].rearrange("t (h d) -> t h d", d=HEAD_DIM),
+                    in_=result[n][b:P:BATCH, :].rearrange("t (h d) -> t h d", d=HEAD_DIM),
                 )
 
         for g in range(first_split_group):

@@ -133,6 +133,11 @@ def tile_selfattention_pa_k_kernel(tc, x, w_qkv_words, w_qkv_scales, out_0, out_
                         .bitcast(I32),
                     )
 
+        def hold_back_words(g, scale_group):
+            nc.vector.tensor_copy(
+                out=w_words[0:4, g, 0:4].bitcast(I32), in_=w_scales[0:4, scale_group, 0:4].bitcast(I32)
+            )
+
         def load_words(g, first_byte, last_byte):
             nc.sync.dma_start(
                 out=w_words[:, g, first_byte:last_byte].bitcast(I32),
@@ -145,14 +150,7 @@ def tile_selfattention_pa_k_kernel(tc, x, w_qkv_words, w_qkv_scales, out_0, out_
                 nc.sync.dma_start(
                     out=x_sb[b:P:BATCH, i * piece : (i + 1) * piece], in_=x[b, :, i * piece : (i + 1) * piece]
                 )
-        first_split_group = GROUPS - SPLIT_GROUPS
-        for first_group in range(0, GROUPS, GROUPS_PER_STRETCH):
-            load_scales(first_group)
-            for g in range(first_group, min(first_group + GROUPS_PER_STRETCH, first_split_group)):
-                load_words(g, 0, ROW_BYTES)
-        for output in range(OUTPUTS):
-            for g in range(first_split_group, GROUPS):
-                load_words(g, output * WORD_BYTES * WIDTH, (output + 1) * WORD_BYTES * WIDTH)
+        load_scales(0)
 
         x_words = x_sb[:].bitcast(F32)
         words_per_group = K_PASS // 2
@@ -176,14 +174,25 @@ def tile_selfattention_pa_k_kernel(tc, x, w_qkv_words, w_qkv_scales, out_0, out_
                 in_=x_grouped[:, these, :].rearrange("p g c -> p (g c)"),
             )
 
-        for first_group in range(0, GROUPS + GROUPS_PER_QUANTISE, GROUPS_PER_QUANTISE):
-            if first_group < GROUPS:
-                transpose_two_groups(first_group, nc.vector.tensor_copy)
-                transpose_two_groups(first_group + 2, nc.scalar.copy)
-            if first_group > 0:
-                quantise(first_group - GROUPS_PER_QUANTISE)
+        for first_group in range(0, GROUPS, 4):
+            transpose_two_groups(first_group, nc.vector.tensor_copy)
+            transpose_two_groups(first_group + 2, nc.scalar.copy)
+        last_scale_dmas = GROUPS_PER_STRETCH - GROUPS_PER_SCALE_DMA
+        hold_back_words(0, last_scale_dmas)
+        for first_group in range(0, GROUPS, GROUPS_PER_QUANTISE):
+            quantise(first_group)
 
+        first_split_group = GROUPS - SPLIT_GROUPS
+        for g in range(GROUPS_PER_STRETCH):
+            load_words(g, 0, ROW_BYTES)
+        load_scales(GROUPS_PER_STRETCH)
         cos_pairs, sin_signed = build_rope_tables(nc, keep)
+        hold_back_words(GROUPS_PER_STRETCH, GROUPS_PER_STRETCH + last_scale_dmas)
+        for g in range(GROUPS_PER_STRETCH, first_split_group):
+            load_words(g, 0, ROW_BYTES)
+        for output in range(OUTPUTS):
+            for g in range(first_split_group, GROUPS):
+                load_words(g, output * WORD_BYTES * WIDTH, (output + 1) * WORD_BYTES * WIDTH)
 
         acc = [psum_acc.tile([P, BANK_COLS], F32, name="acc%d" % n) for n in range(BANKS)]
         result = [keep.tile([P, BANK_COLS], F32, name="result%d" % n) for n in range(BANKS)]

@@ -115,19 +115,23 @@ def tile_selfattention_pa_k_kernel(tc, x, w_qkv_words, w_qkv_scales, out_0, out_
         x_grouped = keep.tile([P, GROUPS, PACK * TOKENS], BF16, align_bytes=64)
         x_codes = keep.tile([P, GROUPS, TOKENS], U32, align_bytes=64)
         x_scales = keep.tile([P, GROUPS, TOKENS], U8, align_bytes=64)
-        w_words = keep.tile([P, GROUPS, ROW_BYTES], U8, align_bytes=64)
-        w_scales = keep.tile([P, GROUPS, N_OUT], U8, align_bytes=64)
+        w_words = [keep.tile([P, ROW_BYTES], U8, align_bytes=64, name="words%d" % g) for g in range(GROUPS)]
+        w_scales = [
+            keep.tile([P, GROUPS_PER_STRETCH, N_OUT], U8, align_bytes=64, name="scales%d" % s)
+            for s in range(GROUPS // GROUPS_PER_STRETCH)
+        ]
         identity = keep.tile([P, P], F32)
         make_identity(nc, identity[:])
 
         def load_scales(first_group):
-            stretch = slice(first_group, first_group + GROUPS_PER_STRETCH)
-            nc.vector.memset(w_scales[:, stretch, :].rearrange("p g n -> p (g n)").bitcast(I32), 0)
-            for g in range(first_group, first_group + GROUPS_PER_STRETCH, GROUPS_PER_SCALE_DMA):
+            planes = w_scales[first_group // GROUPS_PER_STRETCH]
+            nc.vector.memset(planes[:].rearrange("p g n -> p (g n)").bitcast(I32), 0)
+            for i in range(0, GROUPS_PER_STRETCH, GROUPS_PER_SCALE_DMA):
+                g = first_group + i
                 for q in range(8):
                     partition = 32 * (q // 4) + q % 4
                     nc.sync.dma_start(
-                        out=w_scales[partition:P:64, g : g + GROUPS_PER_SCALE_DMA, :].bitcast(I32),
+                        out=planes[partition:P:64, i : i + GROUPS_PER_SCALE_DMA, :].bitcast(I32),
                         in_=w_qkv_scales[g : g + GROUPS_PER_SCALE_DMA, q:16:8, :]
                         .rearrange("g q n -> q g n")
                         .bitcast(I32),
@@ -135,12 +139,13 @@ def tile_selfattention_pa_k_kernel(tc, x, w_qkv_words, w_qkv_scales, out_0, out_
 
         def hold_back_words(g, scale_group):
             nc.vector.tensor_copy(
-                out=w_words[0:4, g, 0:4].bitcast(I32), in_=w_scales[0:4, scale_group, 0:4].bitcast(I32)
+                out=w_words[g][0:4, 0:4].bitcast(I32),
+                in_=w_scales[scale_group // GROUPS_PER_STRETCH][0:4, scale_group % GROUPS_PER_STRETCH, 0:4].bitcast(I32),
             )
 
         def load_words(g, first_byte, last_byte):
             nc.sync.dma_start(
-                out=w_words[:, g, first_byte:last_byte].bitcast(I32),
+                out=w_words[g][:, first_byte:last_byte].bitcast(I32),
                 in_=w_qkv_words[g, :, first_byte:last_byte].bitcast(I32),
             )
 
@@ -202,8 +207,8 @@ def tile_selfattention_pa_k_kernel(tc, x, w_qkv_words, w_qkv_scales, out_0, out_
                 out=acc[n][:],
                 lhsT=x_codes[:, g, :].bitcast(FP8X4),
                 lhsT_scale=x_scales[:, g, :],
-                rhs=w_words[:, g, n * WORD_BYTES * BANK_COLS : (n + 1) * WORD_BYTES * BANK_COLS].bitcast(FP4X4),
-                rhs_scale=w_scales[:, g, n * BANK_COLS : (n + 1) * BANK_COLS],
+                rhs=w_words[g][:, n * WORD_BYTES * BANK_COLS : (n + 1) * WORD_BYTES * BANK_COLS].bitcast(FP4X4),
+                rhs_scale=w_scales[g // GROUPS_PER_STRETCH][:, g % GROUPS_PER_STRETCH, n * BANK_COLS : (n + 1) * BANK_COLS],
                 start=(g == 0),
                 stop=(g == GROUPS - 1),
             )

@@ -37,7 +37,6 @@ ROW_BYTES = WORD_BYTES * N_OUT
 
 X_PIECES = 4
 GROUPS_PER_QUANTISE = 4
-GROUPS_PER_STRETCH = 8
 GROUPS_PER_SCALE_DMA = 4
 SPLIT_GROUPS = 6
 
@@ -117,30 +116,28 @@ def tile_selfattention_pa_k_kernel(tc, x, w_qkv_words, w_qkv_scales, out_0, out_
         x_scales = keep.tile([P, GROUPS, TOKENS], U8, align_bytes=64)
         w_words = [keep.tile([P, ROW_BYTES], U8, align_bytes=64, name="words%d" % g) for g in range(GROUPS)]
         w_scales = [
-            keep.tile([P, GROUPS_PER_STRETCH, N_OUT], U8, align_bytes=64, name="scales%d" % s)
-            for s in range(GROUPS // GROUPS_PER_STRETCH)
+            keep.tile([P, GROUPS_PER_SCALE_DMA, N_OUT], U8, align_bytes=64, name="scales%d" % i)
+            for i in range(GROUPS // GROUPS_PER_SCALE_DMA)
         ]
         identity = keep.tile([P, P], F32)
         make_identity(nc, identity[:])
 
-        def load_scales(first_group):
-            planes = w_scales[first_group // GROUPS_PER_STRETCH]
-            nc.vector.memset(planes[:].rearrange("p g n -> p (g n)").bitcast(I32), 0)
-            for i in range(0, GROUPS_PER_STRETCH, GROUPS_PER_SCALE_DMA):
-                g = first_group + i
+        def load_scales():
+            for i, planes in enumerate(w_scales):
+                engine = nc.gpsimd if i == len(w_scales) - 1 else nc.vector
+                engine.memset(planes[:].rearrange("p g n -> p (g n)").bitcast(I32), 0)
+            for i, planes in enumerate(w_scales):
+                these = slice(i * GROUPS_PER_SCALE_DMA, (i + 1) * GROUPS_PER_SCALE_DMA)
                 for q in range(8):
                     partition = 32 * (q // 4) + q % 4
                     nc.sync.dma_start(
-                        out=planes[partition:P:64, i : i + GROUPS_PER_SCALE_DMA, :].bitcast(I32),
-                        in_=w_qkv_scales[g : g + GROUPS_PER_SCALE_DMA, q:16:8, :]
-                        .rearrange("g q n -> q g n")
-                        .bitcast(I32),
+                        out=planes[partition:P:64, :, :].bitcast(I32),
+                        in_=w_qkv_scales[these, q:16:8, :].rearrange("g q n -> q g n").bitcast(I32),
                     )
 
-        def hold_back_words(g, scale_group):
+        def hold_back_words(g):
             nc.vector.tensor_copy(
-                out=w_words[g][0:4, 0:4].bitcast(I32),
-                in_=w_scales[scale_group // GROUPS_PER_STRETCH][0:4, scale_group % GROUPS_PER_STRETCH, 0:4].bitcast(I32),
+                out=w_words[g][0:4, 0:4].bitcast(I32), in_=w_scales[len(w_scales) - 1][0:4, 0, 0:4].bitcast(I32)
             )
 
         def load_words(g, first_byte, last_byte):
@@ -155,7 +152,7 @@ def tile_selfattention_pa_k_kernel(tc, x, w_qkv_words, w_qkv_scales, out_0, out_
                 nc.sync.dma_start(
                     out=x_sb[b:P:BATCH, i * piece : (i + 1) * piece], in_=x[b, :, i * piece : (i + 1) * piece]
                 )
-        load_scales(0)
+        load_scales()
 
         x_words = x_sb[:].bitcast(F32)
         words_per_group = K_PASS // 2
@@ -182,19 +179,14 @@ def tile_selfattention_pa_k_kernel(tc, x, w_qkv_words, w_qkv_scales, out_0, out_
         for first_group in range(0, GROUPS, 4):
             transpose_two_groups(first_group, nc.vector.tensor_copy)
             transpose_two_groups(first_group + 2, nc.scalar.copy)
-        last_scale_dmas = GROUPS_PER_STRETCH - GROUPS_PER_SCALE_DMA
-        hold_back_words(0, last_scale_dmas)
         for first_group in range(0, GROUPS, GROUPS_PER_QUANTISE):
             quantise(first_group)
+        hold_back_words(0)
 
         first_split_group = GROUPS - SPLIT_GROUPS
-        for g in range(GROUPS_PER_STRETCH):
+        for g in range(first_split_group):
             load_words(g, 0, ROW_BYTES)
-        load_scales(GROUPS_PER_STRETCH)
         cos_pairs, sin_signed = build_rope_tables(nc, keep)
-        hold_back_words(GROUPS_PER_STRETCH, GROUPS_PER_STRETCH + last_scale_dmas)
-        for g in range(GROUPS_PER_STRETCH, first_split_group):
-            load_words(g, 0, ROW_BYTES)
         for output in range(OUTPUTS):
             for g in range(first_split_group, GROUPS):
                 load_words(g, output * WORD_BYTES * WIDTH, (output + 1) * WORD_BYTES * WIDTH)
@@ -208,7 +200,9 @@ def tile_selfattention_pa_k_kernel(tc, x, w_qkv_words, w_qkv_scales, out_0, out_
                 lhsT=x_codes[:, g, :].bitcast(FP8X4),
                 lhsT_scale=x_scales[:, g, :],
                 rhs=w_words[g][:, n * WORD_BYTES * BANK_COLS : (n + 1) * WORD_BYTES * BANK_COLS].bitcast(FP4X4),
-                rhs_scale=w_scales[g // GROUPS_PER_STRETCH][:, g % GROUPS_PER_STRETCH, n * BANK_COLS : (n + 1) * BANK_COLS],
+                rhs_scale=w_scales[g // GROUPS_PER_SCALE_DMA][
+                    :, g % GROUPS_PER_SCALE_DMA, n * BANK_COLS : (n + 1) * BANK_COLS
+                ],
                 start=(g == 0),
                 stop=(g == GROUPS - 1),
             )

@@ -38,7 +38,8 @@ ROW_BYTES = WORD_BYTES * N_OUT
 X_PIECES = 4
 GROUPS_PER_QUANTISE = 4
 GROUPS_PER_SCALE_DMA = 4
-SPLIT_GROUPS = 6
+SPLIT_GROUPS = 8
+TAIL_GROUPS = 3
 
 ROPE_BASE = 10000.0
 ROUND_MAGIC = 1.5 * 2.0**23
@@ -124,9 +125,10 @@ def tile_selfattention_pa_k_kernel(tc, x, w_qkv_words, w_qkv_scales, out_0, out_
 
         def load_scales():
             for i, planes in enumerate(w_scales):
-                engine = nc.gpsimd if i == len(w_scales) - 1 else nc.vector
+                engine = nc.gpsimd if i == 0 else nc.vector
                 engine.memset(planes[:].rearrange("p g n -> p (g n)").bitcast(I32), 0)
-            for i, planes in enumerate(w_scales):
+            for i in (*range(1, len(w_scales)), 0):
+                planes = w_scales[i]
                 these = slice(i * GROUPS_PER_SCALE_DMA, (i + 1) * GROUPS_PER_SCALE_DMA)
                 for q in range(8):
                     partition = 32 * (q // 4) + q % 4
@@ -137,7 +139,7 @@ def tile_selfattention_pa_k_kernel(tc, x, w_qkv_words, w_qkv_scales, out_0, out_
 
         def hold_back_words(g):
             nc.vector.tensor_copy(
-                out=w_words[g][0:4, 0:4].bitcast(I32), in_=w_scales[len(w_scales) - 1][0:4, 0, 0:4].bitcast(I32)
+                out=w_words[g][0:4, 0:4].bitcast(I32), in_=w_scales[0][0:4, 0, 0:4].bitcast(I32)
             )
 
         def load_words(g, first_byte, last_byte):
@@ -147,11 +149,10 @@ def tile_selfattention_pa_k_kernel(tc, x, w_qkv_words, w_qkv_scales, out_0, out_
             )
 
         piece = D_MODEL // X_PIECES
+        x_rows = x.rearrange("b t k -> (b t) k")
         for i in range(X_PIECES):
-            for b in range(BATCH):
-                nc.sync.dma_start(
-                    out=x_sb[b:P:BATCH, i * piece : (i + 1) * piece], in_=x[b, :, i * piece : (i + 1) * piece]
-                )
+            nc.sync.dma_start(out=x_sb[:, i * piece : (i + 1) * piece], in_=x_rows[:, i * piece : (i + 1) * piece])
+        load_words(0, 0, ROW_BYTES)
         load_scales()
 
         x_words = x_sb[:].bitcast(F32)
@@ -164,8 +165,10 @@ def tile_selfattention_pa_k_kernel(tc, x, w_qkv_words, w_qkv_scales, out_0, out_
                 for u in range(2):
                     nc.tensor.transpose(xt[:, i, u, :], x_words[:, start + u : start + words_per_group : 2], identity[:])
             copy(
-                out=x_grouped[:, first_group : first_group + 2, :].bitcast(F32).rearrange("p g (m u) -> p g m u", u=2),
-                in_=xt[:].rearrange("p g u m -> p g m u"),
+                out=x_grouped[:, first_group : first_group + 2, :]
+                .bitcast(F32)
+                .rearrange("p g (t b u) -> p g t b u", b=BATCH, u=2),
+                in_=xt[:].rearrange("p g u (b t) -> p g t b u", b=BATCH),
             )
 
         def quantise(first_group):
@@ -181,15 +184,25 @@ def tile_selfattention_pa_k_kernel(tc, x, w_qkv_words, w_qkv_scales, out_0, out_
             transpose_two_groups(first_group + 2, nc.scalar.copy)
         for first_group in range(0, GROUPS, GROUPS_PER_QUANTISE):
             quantise(first_group)
-        hold_back_words(0)
+        hold_back_words(1)
 
         first_split_group = GROUPS - SPLIT_GROUPS
-        for g in range(first_split_group):
+        first_tail_group = GROUPS - TAIL_GROUPS
+        split_stages = [
+            (0, 2, range(first_split_group, GROUPS)),
+            (2, 2, range(first_split_group, GROUPS)),
+            (4, 2, range(first_split_group, first_tail_group)),
+            (4, 1, range(first_tail_group, GROUPS)),
+            (5, 1, range(first_tail_group, GROUPS)),
+        ]
+        for output in range(OUTPUTS):
+            load_words(1, output * WORD_BYTES * WIDTH, (output + 1) * WORD_BYTES * WIDTH)
+        for g in range(2, first_split_group):
             load_words(g, 0, ROW_BYTES)
         cos_pairs, sin_signed = build_rope_tables(nc, keep)
-        for output in range(OUTPUTS):
-            for g in range(first_split_group, GROUPS):
-                load_words(g, output * WORD_BYTES * WIDTH, (output + 1) * WORD_BYTES * WIDTH)
+        for first_bank, banks, groups in split_stages:
+            for g in groups:
+                load_words(g, first_bank * WORD_BYTES * BANK_COLS, (first_bank + banks) * WORD_BYTES * BANK_COLS)
 
         acc = [psum_acc.tile([P, BANK_COLS], F32, name="acc%d" % n) for n in range(BANKS)]
         result = [keep.tile([P, BANK_COLS], F32, name="result%d" % n) for n in range(BANKS)]
@@ -244,16 +257,15 @@ def tile_selfattention_pa_k_kernel(tc, x, w_qkv_words, w_qkv_scales, out_0, out_
         for g in range(first_split_group):
             for n in range(BANKS):
                 multiply(g, n)
-        for output in range(OUTPUTS):
-            banks = range(output * BANKS_PER_OUTPUT, (output + 1) * BANKS_PER_OUTPUT)
-            for g in range(first_split_group, GROUPS):
-                for n in banks:
+        for first_bank, banks, groups in split_stages:
+            for g in groups:
+                for n in range(first_bank, first_bank + banks):
                     multiply(g, n)
-            for n in banks:
+            if groups[-1] < GROUPS - 1:
+                continue
+            for n in range(first_bank, first_bank + banks):
                 if n < ROTATED_BANKS:
                     rotate(n)
-                elif n % 2 == 0:
-                    nc.scalar.copy(out=result[n][:], in_=acc[n][:])
                 else:
-                    nc.vector.tensor_copy(out=result[n][:], in_=acc[n][:])
+                    nc.scalar.copy(out=result[n][:], in_=acc[n][:])
                 store(n)

@@ -29,8 +29,7 @@ BANK_COLS = 512
 BANKS = N_OUT // BANK_COLS
 BANKS_PER_OUTPUT = WIDTH // BANK_COLS
 HEADS_PER_BANK = BANK_COLS // HEAD_DIM
-ROTATED_BANKS = 2 * BANKS_PER_OUTPUT
-PAIRS = HEAD_DIM // 2
+ROTATED_OUTPUTS = 2
 
 WORD_BYTES = 2
 ROW_BYTES = WORD_BYTES * N_OUT
@@ -38,8 +37,8 @@ ROW_BYTES = WORD_BYTES * N_OUT
 X_PIECES = 4
 GROUPS_PER_QUANTISE = 4
 GROUPS_PER_SCALE_DMA = 4
+EARLY_GROUPS = 2
 SPLIT_GROUPS = 8
-TAIL_GROUPS = 3
 
 ROPE_BASE = 10000.0
 ROUND_MAGIC = 1.5 * 2.0**23
@@ -91,13 +90,13 @@ def build_rope_tables(nc, pool):
         out=cos_arg[:], in0=magnitude[:], scalar1=-1.0, scalar2=math.pi / 2.0, op0=ALU.mult, op1=ALU.add
     )
 
-    cos_pairs = pool.tile([P, HEAD_DIM], F32)
-    nc.scalar.activation(out=cos_pairs[:], in_=cos_arg[:], func=ACT.Sin)
-    sin_signed = pool.tile([P, 2, PAIRS], F32)
-    one_of_each_pair = reduced[:, 0:HEAD_DIM:2]
-    nc.scalar.activation(out=sin_signed[:, 0, :], in_=one_of_each_pair, func=ACT.Sin, scale=-1.0)
-    nc.scalar.activation(out=sin_signed[:, 1, :], in_=one_of_each_pair, func=ACT.Sin)
-    return cos_pairs, sin_signed
+    table = pool.tile([P, 2, HEAD_DIM], F32)
+    nc.scalar.activation(out=table[:, 0, :], in_=cos_arg[:], func=ACT.Sin)
+    for j, sign in enumerate((1.0, -1.0)):
+        nc.scalar.activation(
+            out=table[:, 1, j:HEAD_DIM:2], in_=reduced[:, j:HEAD_DIM:2], func=ACT.Sin, scale=sign
+        )
+    return table
 
 
 def tile_selfattention_pa_k_kernel(tc, x, w_qkv_words, w_qkv_scales, out_0, out_1, out_2):
@@ -124,10 +123,10 @@ def tile_selfattention_pa_k_kernel(tc, x, w_qkv_words, w_qkv_scales, out_0, out_
         make_identity(nc, identity[:])
 
         def load_scales():
-            for i, planes in enumerate(w_scales):
-                engine = nc.gpsimd if i == 0 else nc.vector
-                engine.memset(planes[:].rearrange("p g n -> p (g n)").bitcast(I32), 0)
-            for i in (*range(1, len(w_scales)), 0):
+            order = (1, 2, 0, 3)
+            for i in order:
+                nc.gpsimd.memset(w_scales[i][:].rearrange("p g n -> p (g n)").bitcast(I32), 0)
+            for i in order:
                 planes = w_scales[i]
                 these = slice(i * GROUPS_PER_SCALE_DMA, (i + 1) * GROUPS_PER_SCALE_DMA)
                 for q in range(8):
@@ -139,7 +138,7 @@ def tile_selfattention_pa_k_kernel(tc, x, w_qkv_words, w_qkv_scales, out_0, out_
 
         def hold_back_words(g):
             nc.vector.tensor_copy(
-                out=w_words[g][0:4, 0:4].bitcast(I32), in_=w_scales[0][0:4, 0, 0:4].bitcast(I32)
+                out=w_words[g][0:2, 0:4].bitcast(I32), in_=w_scales[len(w_scales) - 1][0:2, 0, 0:4].bitcast(I32)
             )
 
         def load_words(g, first_byte, last_byte):
@@ -152,7 +151,8 @@ def tile_selfattention_pa_k_kernel(tc, x, w_qkv_words, w_qkv_scales, out_0, out_
         x_rows = x.rearrange("b t k -> (b t) k")
         for i in range(X_PIECES):
             nc.sync.dma_start(out=x_sb[:, i * piece : (i + 1) * piece], in_=x_rows[:, i * piece : (i + 1) * piece])
-        load_words(0, 0, ROW_BYTES)
+        for g in range(EARLY_GROUPS):
+            load_words(g, 0, ROW_BYTES)
         load_scales()
 
         x_words = x_sb[:].bitcast(F32)
@@ -184,25 +184,17 @@ def tile_selfattention_pa_k_kernel(tc, x, w_qkv_words, w_qkv_scales, out_0, out_
             transpose_two_groups(first_group + 2, nc.scalar.copy)
         for first_group in range(0, GROUPS, GROUPS_PER_QUANTISE):
             quantise(first_group)
-        hold_back_words(1)
+        hold_back_words(EARLY_GROUPS)
 
         first_split_group = GROUPS - SPLIT_GROUPS
-        first_tail_group = GROUPS - TAIL_GROUPS
-        split_stages = [
-            (0, 2, range(first_split_group, GROUPS)),
-            (2, 2, range(first_split_group, GROUPS)),
-            (4, 2, range(first_split_group, first_tail_group)),
-            (4, 1, range(first_tail_group, GROUPS)),
-            (5, 1, range(first_tail_group, GROUPS)),
-        ]
         for output in range(OUTPUTS):
-            load_words(1, output * WORD_BYTES * WIDTH, (output + 1) * WORD_BYTES * WIDTH)
-        for g in range(2, first_split_group):
+            load_words(EARLY_GROUPS, output * WORD_BYTES * WIDTH, (output + 1) * WORD_BYTES * WIDTH)
+        for g in range(EARLY_GROUPS + 1, first_split_group):
             load_words(g, 0, ROW_BYTES)
-        cos_pairs, sin_signed = build_rope_tables(nc, keep)
-        for first_bank, banks, groups in split_stages:
-            for g in groups:
-                load_words(g, first_bank * WORD_BYTES * BANK_COLS, (first_bank + banks) * WORD_BYTES * BANK_COLS)
+        rope_table = build_rope_tables(nc, keep)
+        for output in range(OUTPUTS):
+            for g in range(first_split_group, GROUPS):
+                load_words(g, output * WORD_BYTES * WIDTH, (output + 1) * WORD_BYTES * WIDTH)
 
         acc = [psum_acc.tile([P, BANK_COLS], F32, name="acc%d" % n) for n in range(BANKS)]
         result = [keep.tile([P, BANK_COLS], F32, name="result%d" % n) for n in range(BANKS)]
@@ -220,30 +212,26 @@ def tile_selfattention_pa_k_kernel(tc, x, w_qkv_words, w_qkv_scales, out_0, out_
                 stop=(g == GROUPS - 1),
             )
 
-        def rotate(n):
-            by_head = "p (h d) -> p h d"
-            cos_part = work.tile([P, BANK_COLS], F32)
-            nc.vector.tensor_tensor(
-                out=cos_part[:].rearrange(by_head, d=HEAD_DIM),
-                in0=acc[n][:].rearrange(by_head, d=HEAD_DIM),
-                in1=cos_pairs[:].unsqueeze(1).to_broadcast([P, HEADS_PER_BANK, HEAD_DIM]),
-                op=ALU.mult,
-            )
-            u_planes = acc[n][:].rearrange("p (c j) -> p j c", j=2)
-            sin_part = work.tile([P, 2, BANK_COLS // 2], F32)
-            for j in range(2):
+        def rotate(banks):
+            shape = [P, 2, HEADS_PER_BANK, HEAD_DIM]
+            products = []
+            for n in banks:
+                product = work.tile([P, 2, BANK_COLS], F32)
                 nc.vector.tensor_tensor(
-                    out=sin_part[:, j, :].rearrange(by_head, d=PAIRS),
-                    in0=u_planes[:, 1 - j, :].rearrange(by_head, d=PAIRS),
-                    in1=sin_signed[:, j, :].unsqueeze(1).to_broadcast([P, HEADS_PER_BANK, PAIRS]),
+                    out=product[:].rearrange("p s (h d) -> p s h d", d=HEAD_DIM),
+                    in0=acc[n][:].rearrange("p (h d) -> p h d", d=HEAD_DIM).unsqueeze(1).to_broadcast(shape),
+                    in1=rope_table[:].unsqueeze(2).to_broadcast(shape),
                     op=ALU.mult,
                 )
-            nc.vector.tensor_tensor(
-                out=result[n][:].rearrange("p (c j) -> p c j", j=2),
-                in0=cos_part[:].rearrange("p (c j) -> p c j", j=2),
-                in1=sin_part[:].rearrange("p j c -> p c j"),
-                op=ALU.add,
-            )
+                products.append(product)
+            pairs = "p (c j) -> p c j"
+            for n, product in zip(banks, products):
+                nc.vector.tensor_tensor(
+                    out=result[n][:].rearrange(pairs, j=2),
+                    in0=product[:, 0, :].rearrange(pairs, j=2),
+                    in1=product[:, 1, :].rearrange(pairs, j=2)[:, :, ::-1],
+                    op=ALU.add,
+                )
 
         def store(n):
             output, half = divmod(n, BANKS_PER_OUTPUT)
@@ -257,15 +245,15 @@ def tile_selfattention_pa_k_kernel(tc, x, w_qkv_words, w_qkv_scales, out_0, out_
         for g in range(first_split_group):
             for n in range(BANKS):
                 multiply(g, n)
-        for first_bank, banks, groups in split_stages:
-            for g in groups:
-                for n in range(first_bank, first_bank + banks):
+        for output in range(OUTPUTS):
+            banks = range(output * BANKS_PER_OUTPUT, (output + 1) * BANKS_PER_OUTPUT)
+            for g in range(first_split_group, GROUPS):
+                for n in banks:
                     multiply(g, n)
-            if groups[-1] < GROUPS - 1:
-                continue
-            for n in range(first_bank, first_bank + banks):
-                if n < ROTATED_BANKS:
-                    rotate(n)
-                else:
-                    nc.scalar.copy(out=result[n][:], in_=acc[n][:])
+            if output < ROTATED_OUTPUTS:
+                rotate(banks)
+            else:
+                nc.scalar.copy(out=result[banks[0]][:], in_=acc[banks[0]][:])
+                nc.vector.tensor_copy(out=result[banks[1]][:], in_=acc[banks[1]][:])
+            for n in banks:
                 store(n)

@@ -36,8 +36,8 @@ ROW_BYTES = WORD_BYTES * N_OUT
 
 X_PIECES = 4
 GROUPS_PER_QUANTISE = 4
-GROUPS_PER_SCALE_DMA = 4
-EARLY_GROUPS = 2
+GROUPS_PER_SCALE_DMA = 8
+EARLY_GROUPS = 4
 SPLIT_GROUPS = 8
 
 ROPE_BASE = 10000.0
@@ -123,10 +123,9 @@ def tile_selfattention_pa_k_kernel(tc, x, w_qkv_words, w_qkv_scales, out_0, out_
         make_identity(nc, identity[:])
 
         def load_scales():
-            order = (1, 2, 0, 3)
-            for i in order:
+            for i in range(len(w_scales)):
                 nc.gpsimd.memset(w_scales[i][:].rearrange("p g n -> p (g n)").bitcast(I32), 0)
-            for i in order:
+            for i in range(len(w_scales)):
                 planes = w_scales[i]
                 these = slice(i * GROUPS_PER_SCALE_DMA, (i + 1) * GROUPS_PER_SCALE_DMA)
                 for q in range(8):
@@ -138,7 +137,7 @@ def tile_selfattention_pa_k_kernel(tc, x, w_qkv_words, w_qkv_scales, out_0, out_
 
         def hold_back_words(g):
             nc.vector.tensor_copy(
-                out=w_words[g][0:2, 0:4].bitcast(I32), in_=w_scales[len(w_scales) - 1][0:2, 0, 0:4].bitcast(I32)
+                out=w_words[g][32:33, 0:4].bitcast(I32), in_=w_scales[len(w_scales) - 1][32:33, 0, 0:4].bitcast(I32)
             )
 
         def load_words(g, first_byte, last_byte):

@@ -111,12 +111,12 @@ def tile_selfattention_pa_k_kernel(tc, x, w_qkv_words, w_qkv_scales, out_0, out_
         psum_acc = ctx.enter_context(tc.psum_pool(name="psum_acc", bufs=1))
 
         x_sb = keep.tile([P, D_MODEL], BF16)
-        x_grouped = keep.tile([P, GROUPS, PACK * TOKENS], BF16, align_bytes=64)
-        x_codes = keep.tile([P, GROUPS, TOKENS], U32, align_bytes=64)
-        x_scales = keep.tile([P, GROUPS, TOKENS], U8, align_bytes=64)
-        w_words = [keep.tile([P, ROW_BYTES], U8, align_bytes=64, name="words%d" % g) for g in range(GROUPS)]
+        x_grouped = keep.tile([P, GROUPS, PACK * TOKENS], BF16, align_bytes=256)
+        x_codes = keep.tile([P, GROUPS, TOKENS], U32, align_bytes=256)
+        x_scales = keep.tile([P, GROUPS, TOKENS], U8, align_bytes=256)
+        w_words = [keep.tile([P, ROW_BYTES], U8, align_bytes=256, name="words%d" % g) for g in range(GROUPS)]
         w_scales = [
-            keep.tile([P, GROUPS_PER_SCALE_DMA, N_OUT], U8, align_bytes=64, name="scales%d" % i)
+            keep.tile([P, GROUPS_PER_SCALE_DMA, N_OUT], U8, align_bytes=256, name="scales%d" % i)
             for i in range(GROUPS // GROUPS_PER_SCALE_DMA)
         ]
         identity = keep.tile([P, P], F32)

@@ -38,7 +38,7 @@ X_PIECES = 4
 GROUPS_PER_QUANTISE = 4
 GROUPS_PER_SCALE_DMA = 8
 EARLY_GROUPS = 4
-SPLIT_GROUPS = 8
+SPLIT_GROUPS = 6
 
 ROPE_BASE = 10000.0
 ROUND_MAGIC = 1.5 * 2.0**23
@@ -110,7 +110,7 @@ def tile_selfattention_pa_k_kernel(tc, x, w_qkv_words, w_qkv_scales, out_0, out_
         psum_xt = ctx.enter_context(tc.psum_pool(name="psum_xt", bufs=2))
         psum_acc = ctx.enter_context(tc.psum_pool(name="psum_acc", bufs=1))
 
-        x_sb = keep.tile([P, D_MODEL], BF16)
+        x_sb = keep.tile([P, D_MODEL], BF16, align_bytes=256)
         x_grouped = keep.tile([P, GROUPS, PACK * TOKENS], BF16, align_bytes=256)
         x_codes = keep.tile([P, GROUPS, TOKENS], U32, align_bytes=256)
         x_scales = keep.tile([P, GROUPS, TOKENS], U8, align_bytes=256)
@@ -196,7 +196,7 @@ def tile_selfattention_pa_k_kernel(tc, x, w_qkv_words, w_qkv_scales, out_0, out_
                 load_words(g, output * WORD_BYTES * WIDTH, (output + 1) * WORD_BYTES * WIDTH)
 
         acc = [psum_acc.tile([P, BANK_COLS], F32, name="acc%d" % n) for n in range(BANKS)]
-        result = [keep.tile([P, BANK_COLS], F32, name="result%d" % n) for n in range(BANKS)]
+        result = [keep.tile([P, BANK_COLS], F32, align_bytes=256, name="result%d" % n) for n in range(BANKS)]
 
         def multiply(g, n):
             nc.tensor.matmul_mx(

import math
from contextlib import ExitStack

import concourse.mybir as mybir
from concourse.masks import make_identity

F32 = mybir.dt.float32
BF16 = mybir.dt.bfloat16
I32 = mybir.dt.int32
U32 = mybir.dt.uint32
U8 = mybir.dt.uint8
FP8X4 = mybir.dt.float8_e4m3fn_x4
FP4X4 = mybir.dt.float4_e2m1fn_x4
ALU = mybir.AluOpType
ACT = mybir.ActivationFunctionType

P = 128
PACK = 4
K_PASS = P * PACK

BATCH, SEQ, D_MODEL, HEADS, HEAD_DIM = 2, 64, 8192, 8, 128
TOKENS = BATCH * SEQ
WIDTH = HEADS * HEAD_DIM
OUTPUTS = 3
N_OUT = OUTPUTS * WIDTH
GROUPS = D_MODEL // K_PASS

BANK_COLS = 512
BANKS = N_OUT // BANK_COLS
BANKS_PER_OUTPUT = WIDTH // BANK_COLS
HEADS_PER_BANK = BANK_COLS // HEAD_DIM
ROTATED_OUTPUTS = 2

WORD_BYTES = 2
ROW_BYTES = WORD_BYTES * N_OUT

X_PIECES = 4
GROUPS_PER_QUANTISE = 4
GROUPS_PER_SCALE_DMA = 8
EARLY_GROUPS = 4
SPLIT_GROUPS = 6

ROPE_BASE = 10000.0
ROUND_MAGIC = 1.5 * 2.0**23
TWO_PI_HIGH = 6.28125
TWO_PI_LOW = 2.0 * math.pi - TWO_PI_HIGH

FLOPS = 2 * TOKENS * D_MODEL * N_OUT


def build_rope_tables(nc, pool):
    freq = pool.tile([P, HEAD_DIM], F32)
    nc.vector.memset(freq[:, 0:2], 1.0)
    done = 2
    while done < HEAD_DIM:
        ratio = ROPE_BASE ** (-float(done) / HEAD_DIM)
        nc.vector.tensor_scalar_mul(out=freq[:, done : 2 * done], in0=freq[:, 0:done], scalar1=ratio)
        done *= 2

    partition_index = pool.tile([P, 1], I32)
    nc.gpsimd.iota(partition_index[:], pattern=[[0, 1]], base=0, channel_multiplier=1)
    position_int = pool.tile([P, 1], I32)
    nc.vector.tensor_single_scalar(out=position_int[:], in_=partition_index[:], scalar=1, op=ALU.logical_shift_right)
    position = pool.tile([P, 1], F32)
    nc.vector.tensor_copy(out=position[:], in_=position_int[:])

    angle = pool.tile([P, HEAD_DIM], F32)
    nc.vector.tensor_scalar_mul(out=angle[:], in0=freq[:], scalar1=position[:, 0:1])

    shifted = pool.tile([P, HEAD_DIM], F32)
    nc.vector.tensor_scalar(
        out=shifted[:], in0=angle[:], scalar1=1.0 / (2.0 * math.pi), scalar2=ROUND_MAGIC, op0=ALU.mult, op1=ALU.add
    )
    turns = pool.tile([P, HEAD_DIM], F32)
    nc.vector.tensor_scalar_sub(out=turns[:], in0=shifted[:], scalar1=ROUND_MAGIC)
    coarse = pool.tile([P, HEAD_DIM], F32)
    nc.vector.scalar_tensor_tensor(
        out=coarse[:], in0=turns[:], scalar=-TWO_PI_HIGH, in1=angle[:], op0=ALU.mult, op1=ALU.add
    )
    reduced = pool.tile([P, HEAD_DIM], F32)
    nc.vector.scalar_tensor_tensor(
        out=reduced[:], in0=turns[:], scalar=-TWO_PI_LOW, in1=coarse[:], op0=ALU.mult, op1=ALU.add
    )
    magnitude = pool.tile([P, HEAD_DIM], F32)
    nc.vector.scalar_tensor_tensor(
        out=magnitude[:], in0=reduced[:], scalar=-1.0, in1=reduced[:], op0=ALU.mult, op1=ALU.max
    )
    cos_arg = pool.tile([P, HEAD_DIM], F32)
    nc.vector.tensor_scalar(
        out=cos_arg[:], in0=magnitude[:], scalar1=-1.0, scalar2=math.pi / 2.0, op0=ALU.mult, op1=ALU.add
    )

    table = pool.tile([P, 2, HEAD_DIM], F32)
    nc.scalar.activation(out=table[:, 0, :], in_=cos_arg[:], func=ACT.Sin)
    for j, sign in enumerate((1.0, -1.0)):
        nc.scalar.activation(
            out=table[:, 1, j:HEAD_DIM:2], in_=reduced[:, j:HEAD_DIM:2], func=ACT.Sin, scale=sign
        )
    return table


def tile_selfattention_pa_k_kernel(tc, x, w_qkv_words, w_qkv_scales, out_0, out_1, out_2):
    nc = tc.nc
    outs = (out_0, out_1, out_2)

    with ExitStack() as ctx:
        ctx.enter_context(tc.manual_schedule())
        keep = ctx.enter_context(tc.tile_pool(name="keep", bufs=1))
        work = ctx.enter_context(tc.tile_pool(name="work", bufs=2))
        psum_xt = ctx.enter_context(tc.psum_pool(name="psum_xt", bufs=2))
        psum_acc = ctx.enter_context(tc.psum_pool(name="psum_acc", bufs=1))

        x_sb = keep.tile([P, D_MODEL], BF16, align_bytes=256)
        x_grouped = keep.tile([P, GROUPS, PACK * TOKENS], BF16, align_bytes=256)
        x_codes = keep.tile([P, GROUPS, TOKENS], U32, align_bytes=256)
        x_scales = keep.tile([P, GROUPS, TOKENS], U8, align_bytes=256)
        w_words = [keep.tile([P, ROW_BYTES], U8, align_bytes=256, name="words%d" % g) for g in range(GROUPS)]
        w_scales = [
            keep.tile([P, GROUPS_PER_SCALE_DMA, N_OUT], U8, align_bytes=256, name="scales%d" % i)
            for i in range(GROUPS // GROUPS_PER_SCALE_DMA)
        ]
        identity = keep.tile([P, P], F32)
        make_identity(nc, identity[:])

        def load_scales():
            for i in range(len(w_scales)):
                nc.gpsimd.memset(w_scales[i][:].rearrange("p g n -> p (g n)").bitcast(I32), 0)
            for i in range(len(w_scales)):
                planes = w_scales[i]
                these = slice(i * GROUPS_PER_SCALE_DMA, (i + 1) * GROUPS_PER_SCALE_DMA)
                for q in range(8):
                    partition = 32 * (q // 4) + q % 4
                    nc.sync.dma_start(
                        out=planes[partition:P:64, :, :].bitcast(I32),
                        in_=w_qkv_scales[these, q:16:8, :].rearrange("g q n -> q g n").bitcast(I32),
                    )

        def hold_back_words(g):
            nc.vector.tensor_copy(
                out=w_words[g][32:33, 0:4].bitcast(I32), in_=w_scales[len(w_scales) - 1][32:33, 0, 0:4].bitcast(I32)
            )

        def load_words(g, first_byte, last_byte):
            nc.sync.dma_start(
                out=w_words[g][:, first_byte:last_byte].bitcast(I32),
                in_=w_qkv_words[g, :, first_byte:last_byte].bitcast(I32),
            )

        piece = D_MODEL // X_PIECES
        x_rows = x.rearrange("b t k -> (b t) k")
        for i in range(X_PIECES):
            nc.sync.dma_start(out=x_sb[:, i * piece : (i + 1) * piece], in_=x_rows[:, i * piece : (i + 1) * piece])
        for g in range(EARLY_GROUPS):
            load_words(g, 0, ROW_BYTES)
        load_scales()

        x_words = x_sb[:].bitcast(F32)
        words_per_group = K_PASS // 2

        def transpose_two_groups(first_group, copy):
            xt = psum_xt.tile([P, 2, 2, TOKENS], F32)
            for i in range(2):
                start = (first_group + i) * words_per_group
                for u in range(2):
                    nc.tensor.transpose(xt[:, i, u, :], x_words[:, start + u : start + words_per_group : 2], identity[:])
            copy(
                out=x_grouped[:, first_group : first_group + 2, :]
                .bitcast(F32)
                .rearrange("p g (t b u) -> p g t b u", b=BATCH, u=2),
                in_=xt[:].rearrange("p g u (b t) -> p g t b u", b=BATCH),
            )

        def quantise(first_group):
            these = slice(first_group, first_group + GROUPS_PER_QUANTISE)
            nc.vector.quantize_mx(
                out=x_codes[:, these, :].rearrange("p g m -> p (g m)").bitcast(FP8X4),
                scales=x_scales[:, these, :].rearrange("p g m -> p (g m)"),
                in_=x_grouped[:, these, :].rearrange("p g c -> p (g c)"),
            )

        for first_group in range(0, GROUPS, 4):
            transpose_two_groups(first_group, nc.vector.tensor_copy)
            transpose_two_groups(first_group + 2, nc.scalar.copy)
        for first_group in range(0, GROUPS, GROUPS_PER_QUANTISE):
            quantise(first_group)
        hold_back_words(EARLY_GROUPS)

        first_split_group = GROUPS - SPLIT_GROUPS
        for output in range(OUTPUTS):
            load_words(EARLY_GROUPS, output * WORD_BYTES * WIDTH, (output + 1) * WORD_BYTES * WIDTH)
        for g in range(EARLY_GROUPS + 1, first_split_group):
            load_words(g, 0, ROW_BYTES)
        rope_table = build_rope_tables(nc, keep)
        for output in range(OUTPUTS):
            for g in range(first_split_group, GROUPS):
                load_words(g, output * WORD_BYTES * WIDTH, (output + 1) * WORD_BYTES * WIDTH)

        acc = [psum_acc.tile([P, BANK_COLS], F32, name="acc%d" % n) for n in range(BANKS)]
        result = [keep.tile([P, BANK_COLS], F32, align_bytes=256, name="result%d" % n) for n in range(BANKS)]

        def multiply(g, n):
            nc.tensor.matmul_mx(
                out=acc[n][:],
                lhsT=x_codes[:, g, :].bitcast(FP8X4),
                lhsT_scale=x_scales[:, g, :],
                rhs=w_words[g][:, n * WORD_BYTES * BANK_COLS : (n + 1) * WORD_BYTES * BANK_COLS].bitcast(FP4X4),
                rhs_scale=w_scales[g // GROUPS_PER_SCALE_DMA][
                    :, g % GROUPS_PER_SCALE_DMA, n * BANK_COLS : (n + 1) * BANK_COLS
                ],
                start=(g == 0),
                stop=(g == GROUPS - 1),
            )

        def rotate(banks):
            shape = [P, 2, HEADS_PER_BANK, HEAD_DIM]
            products = []
            for n in banks:
                product = work.tile([P, 2, BANK_COLS], F32)
                nc.vector.tensor_tensor(
                    out=product[:].rearrange("p s (h d) -> p s h d", d=HEAD_DIM),
                    in0=acc[n][:].rearrange("p (h d) -> p h d", d=HEAD_DIM).unsqueeze(1).to_broadcast(shape),
                    in1=rope_table[:].unsqueeze(2).to_broadcast(shape),
                    op=ALU.mult,
                )
                products.append(product)
            pairs = "p (c j) -> p c j"
            for n, product in zip(banks, products):
                nc.vector.tensor_tensor(
                    out=result[n][:].rearrange(pairs, j=2),
                    in0=product[:, 0, :].rearrange(pairs, j=2),
                    in1=product[:, 1, :].rearrange(pairs, j=2)[:, :, ::-1],
                    op=ALU.add,
                )

        def store(n):
            output, half = divmod(n, BANKS_PER_OUTPUT)
            heads = slice(half * HEADS_PER_BANK, (half + 1) * HEADS_PER_BANK)
            for b in range(BATCH):
                nc.sync.dma_start(
                    out=outs[output][b, heads].rearrange("h t d -> t h d"),
                    in_=result[n][b:P:BATCH, :].rearrange("t (h d) -> t h d", d=HEAD_DIM),
                )

        for g in range(first_split_group):
            for n in range(BANKS):
                multiply(g, n)
        for output in range(OUTPUTS):
            banks = range(output * BANKS_PER_OUTPUT, (output + 1) * BANKS_PER_OUTPUT)
            for g in range(first_split_group, GROUPS):
                for n in banks:
                    multiply(g, n)
            if output < ROTATED_OUTPUTS:
                rotate(banks)
            else:
                nc.scalar.copy(out=result[banks[0]][:], in_=acc[banks[0]][:])
                nc.vector.tensor_copy(out=result[banks[1]][:], in_=acc[banks[1]][:])
            for n in banks:
                store(n)
